import numpy as np
import ml_dtypes


def mxq(x, axis, fmt="e4m3"):
    dtype, down = {"e4m3": (ml_dtypes.float8_e4m3fn, 7), "e5m2": (ml_dtypes.float8_e5m2, 14)}[fmt]
    v = np.moveaxis(np.asarray(x, np.float32).astype(ml_dtypes.bfloat16).astype(np.float64), axis, -1)
    blocks = v.reshape(v.shape[:-1] + (-1, 32))
    amax = np.abs(blocks).max(-1, keepdims=True)
    byte = np.maximum(np.where(amax > 0, np.frexp(amax)[1] - 1 + 127, 0) - down, 1)
    scale = np.exp2(byte - 127.0)
    codes = (blocks / scale).astype(np.float32).astype(dtype).astype(np.float64)
    return np.moveaxis((codes * scale).reshape(v.shape), -1, axis)


WIDE = False


def mx_kscale(k):
    if not WIDE:
        return np.ones(k)
    levels = np.array([10, -10, 5, -5, 0])
    if k % 512:
        return np.exp2(np.random.permutation(np.resize(levels, k // 32))).repeat(32)
    a = np.empty((k // 512, 16))
    for p in range(k // 512):
        a[p, :8] = np.random.permutation(np.resize(levels, 8))
        for g in range(8):
            far = levels[np.abs(levels - a[p, g]) >= 10]
            a[p, g + 8] = far[np.random.randint(len(far))]
    return np.exp2(a.ravel()).repeat(32)


BF16 = ml_dtypes.bfloat16


def bf(x):
    return np.asarray(x, np.float32).astype(BF16)


def f64(x):
    return np.asarray(x).astype(np.float64)


B, D0, D1, D2, D3, D4 = 512, 1024, 2048, 2048, 1024, 256
DENSITY = 0.02


def setup_inputs():
    s, t = mx_kscale(D0), mx_kscale(D1)
    bound0 = np.sqrt(3.0 / (DENSITY * D0))
    bound1 = np.sqrt(6.0 / (DENSITY * D1))
    return {"x": bf(np.random.standard_normal((B, D0)) * s),
            "W0": bf(np.random.uniform(-bound0, bound0, (D1, D0)) / s[None, :] * t[:, None]),
            "b0": bf(np.random.standard_normal(D1) * 0.3 * t),
            "m0": bf(np.random.uniform(size=(D1, D0)) < DENSITY),
            "W1": bf(np.random.uniform(-bound1, bound1, (D2, D1)) / t[None, :]),
            "b1": bf(np.random.standard_normal(D2) * 0.3),
            "m1": bf(np.random.uniform(size=(D2, D1)) < DENSITY)}


def reference(x, W0, b0, m0, W1, b1, m1):
    h = f64(x).reshape(x.shape[0], -1)
    w0 = f64(W0) * f64(m0)
    pre0 = (mxq(h, 1, "e4m3") @ mxq(w0, 1, "e4m3").T) + f64(b0)
    h0 = np.maximum(pre0, 0.0)
    w1 = f64(W1) * f64(m1)
    pre1 = (mxq(h0, 1, "e4m3") @ mxq(w1, 1, "e4m3").T) + f64(b1)
    return np.maximum(pre1, 0.0)

@@ -1,0 +1,248 @@
+from contextlib import ExitStack
+
+import concourse.mybir as mybir
+from concourse.masks import make_identity
+
+F32 = mybir.dt.float32
+BF16 = mybir.dt.bfloat16
+U32 = mybir.dt.uint32
+U8 = mybir.dt.uint8
+FP8X4 = mybir.dt.float8_e4m3fn_x4
+MULT = mybir.AluOpType.mult
+ADD = mybir.AluOpType.add
+RELU = mybir.ActivationFunctionType.Relu
+
+P = 128
+PACK = 4
+K_PASS = P * PACK
+BANK = 512
+BATCH, D0, D1, D2 = 512, 1024, 2048, 2048
+PASSES0 = D0 // K_PASS
+PASSES1 = D1 // K_PASS
+BATCH_TILES = BATCH // P
+UNIT = 2048
+ROWS0 = P * UNIT // D0
+ROWS1 = P * UNIT // D1
+UNITS0 = D1 // ROWS0
+UNITS = UNITS0 + D2 // ROWS1
+UNITS1 = D2 // ROWS1
+
+LAG_TRANSPOSE = 1
+LAG_QUANTISE = 3
+LAG_MATMUL0 = 3
+LAG_FINISH0 = 5
+LAG_MATMUL1 = 4
+LAG_FINISH1 = 7
+AHEAD = 10
+
+FLOPS = 2 * BATCH * D0 * D1 + 2 * BATCH * D1 * D2
+
+
+def tile_patchedsparsenetwork_pa_kernel(tc, x, W0, b0, m0, W1, b1, m1, out):
+    nc = tc.nc
+    with ExitStack() as ctx:
+        ctx.enter_context(tc.manual_schedule())
+        const = ctx.enter_context(tc.tile_pool(name="const", bufs=1))
+        weights = ctx.enter_context(tc.tile_pool(name="weights", bufs=AHEAD + LAG_TRANSPOSE + 1))
+        grouped_pool = ctx.enter_context(
+            tc.tile_pool(name="grouped", bufs=LAG_QUANTISE - LAG_TRANSPOSE + 2)
+        )
+        codes_pool = ctx.enter_context(
+            tc.tile_pool(name="codes", bufs=LAG_MATMUL1 - LAG_QUANTISE + 2)
+        )
+        h_pool = ctx.enter_context(tc.tile_pool(name="h", bufs=2))
+        tr_psum = ctx.enter_context(tc.psum_pool(name="tr_psum", bufs=4))
+        acc_psum = ctx.enter_context(tc.psum_pool(name="acc_psum", bufs=4))
+
+        w_of, m_of, grouped_of, codes_of, scales_of, acc_of = {}, {}, {}, {}, {}, {}
+        h_rows_of = {}
+
+        def load(i):
+            w = weights.tile([P, UNIT], BF16, tag="w")
+            m = weights.tile([P, UNIT], BF16, tag="m")
+            if i < UNITS0:
+                g, u = divmod(i, 2)
+                rows = slice(K_PASS * g, K_PASS * (g + 1))
+                w_rows = W0[rows, :].rearrange("(q u e) k -> u q (e k)", u=2, e=2)
+                m_rows = m0[rows, :].rearrange("(q u e) k -> u q (e k)", u=2, e=2)
+                nc.sync.dma_start(out=w[:], in_=w_rows[u])
+                nc.sync.dma_start(out=m[:], in_=m_rows[u])
+            else:
+                rows = slice(ROWS1 * (i - UNITS0), ROWS1 * (i - UNITS0 + 1))
+                nc.sync.dma_start(out=w[:], in_=W1[rows, :])
+                nc.sync.dma_start(out=m[:], in_=m1[rows, :])
+            w_of[i], m_of[i] = w, m
+
+        def multiply(i):
+            nc.vector.tensor_tensor(out=w_of[i][:], in0=w_of[i][:], in1=m_of[i][:], op=MULT)
+
+        def transpose(i):
+            w_words = w_of[i][:].bitcast(F32)
+            grouped = grouped_pool.tile([P, UNIT], BF16, tag="grouped", align_bytes=64)
+            grouped_words = grouped[:].bitcast(F32).rearrange(
+                "p (a c q u) -> p a c q u", a=2, c=2, u=2
+            )
+            for a in range(2):
+                bank = tr_psum.tile([P, 4, P], F32, tag="tr")
+                for s in range(4):
+                    c, u = divmod(4 * a + s, 2)
+                    words = slice(2 * P * c + u, 2 * P * (c + 1), 2)
+                    nc.tensor.transpose(bank[:, s, :], w_words[:, words], ident[:])
+                nc.scalar.copy(
+                    out=grouped_words[:, a], in_=bank[:].rearrange("p (c u) q -> p c q u", u=2)
+                )
+            grouped_of[i] = grouped
+
+        def quantise(i):
+            codes = codes_pool.tile([P, UNIT // PACK], U32, tag="codes", align_bytes=64)
+            scales = codes_pool.tile([P, UNIT // PACK], U8, tag="scales", align_bytes=64)
+            nc.vector.quantize_mx(
+                out=codes[:].bitcast(FP8X4), scales=scales[:], in_=grouped_of[i][:]
+            )
+            codes_of[i], scales_of[i] = codes, scales
+
+        def layer0_matmuls(j):
+            g, u = divmod(j, 2)
+            if u == 0:
+                h_rows = h_pool.tile([P, PACK, BATCH], BF16, tag="h_rows")
+                h_rows_of[g] = h_rows
+            for e in range(2):
+                acc = acc_psum.tile([P, BATCH], F32, tag="acc")
+                for g0 in range(PASSES0):
+                    w_cols = slice(P * (PASSES0 * e + g0), P * (PASSES0 * e + g0 + 1))
+                    x_cols = slice(BATCH * g0, BATCH * (g0 + 1))
+                    nc.tensor.matmul_mx(
+                        out=acc[:],
+                        lhsT=codes_of[j][:, w_cols].bitcast(FP8X4),
+                        lhsT_scale=scales_of[j][:, w_cols],
+                        rhs=x_codes[:, x_cols].bitcast(FP8X4),
+                        rhs_scale=x_scales[:, x_cols],
+                        start=(g0 == 0),
+                        stop=(g0 == PASSES0 - 1),
+                    )
+                nc.scalar.activation(
+                    out=h_rows_of[g][:, 2 * u + e, :],
+                    in_=acc[:],
+                    func=RELU,
+                    bias=b0_cols[:, 2 * j + e : 2 * j + e + 1],
+                )
+
+        def layer0_finish(j):
+            g, u = divmod(j, 2)
+            if u == 1:
+                h_grouped = h_pool.tile([P, BATCH, PACK], BF16, tag="h_grouped", align_bytes=64)
+                nc.vector.tensor_copy(
+                    out=h_grouped[:].rearrange("p (c i) t -> p c t i", i=4),
+                    in_=h_rows_of[g][:].rearrange("p t (c i) -> p c t i", i=4),
+                )
+                h_cols = slice(BATCH * g, BATCH * (g + 1))
+                nc.vector.quantize_mx(
+                    out=h_codes[:, h_cols].bitcast(FP8X4),
+                    scales=h_scales[:, h_cols],
+                    in_=h_grouped[:].rearrange("p n t -> p (n t)"),
+                )
+
+        def layer1_matmuls(k):
+            acc = acc_psum.tile([P, BATCH_TILES, ROWS1], F32, tag="acc")
+            for r in range(BATCH_TILES):
+                for g in range(PASSES1):
+                    h_cols = slice(BATCH * g + P * r, BATCH * g + P * (r + 1))
+                    w_cols = slice(ROWS1 * g, ROWS1 * (g + 1))
+                    nc.tensor.matmul_mx(
+                        out=acc[:, r, :],
+                        lhsT=h_codes[:, h_cols].bitcast(FP8X4),
+                        lhsT_scale=h_scales[:, h_cols],
+                        rhs=codes_of[UNITS0 + k][:, w_cols].bitcast(FP8X4),
+                        rhs_scale=scales_of[UNITS0 + k][:, w_cols],
+                        start=(g == 0),
+                        stop=(g == PASSES1 - 1),
+                    )
+            acc_of[k] = acc
+
+        def layer1_finish(k):
+            part = out_rows[:, :, ROWS1 * k : ROWS1 * (k + 1)]
+            bias = b1_all[:, ROWS1 * k : ROWS1 * (k + 1)].unsqueeze(1)
+            nc.vector.tensor_tensor(
+                out=part, in0=acc_of[k][:], in1=bias.to_broadcast([P, BATCH_TILES, ROWS1]), op=ADD
+            )
+            nc.scalar.activation(out=part, in_=part, func=RELU)
+            nc.sync.dma_start(out=out_view[:, :, ROWS1 * k : ROWS1 * (k + 1)], in_=part)
+
+        x_rows = const.tile([P, BATCH_TILES * D0], BF16)
+        nc.sync.dma_start(out=x_rows[:], in_=x.rearrange("(q r) k -> q (r k)", r=BATCH_TILES))
+        out_view = out.rearrange("(q r) d -> q r d", r=BATCH_TILES)
+        out_rows = const.tile([P, BATCH_TILES, D2], F32)
+
+        b0_rows = const.tile([P, K_PASS], BF16)
+        b1_row = const.tile([P, D2], BF16)
+        ones = const.tile([P, P], BF16)
+        nc.vector.memset(b0_rows[:], 0.0)
+        nc.vector.memset(b1_row[:], 0.0)
+        nc.vector.memset(ones[:], 1.0)
+        nc.sync.dma_start(out=b0_rows[0:PASSES1, :], in_=b0.rearrange("(g c) -> g c", c=K_PASS))
+        nc.sync.dma_start(out=b1_row[0:1, :], in_=b1.rearrange("(o d) -> o d", o=1))
+        for i in range(AHEAD):
+            load(i)
+
+        ident = const.tile([P, P], F32)
+        make_identity(nc, ident[:])
+
+        x_words = x_rows[:].bitcast(F32).rearrange("q (r w) -> q r w", r=BATCH_TILES)
+        x_grouped = const.tile([P, PASSES0 * BATCH * PACK], BF16, align_bytes=64)
+        x_grouped_words = x_grouped[:].bitcast(F32).rearrange(
+            "p (g r q u) -> p g r q u", g=PASSES0, r=BATCH_TILES, u=2
+        )
+        for r in range(BATCH_TILES):
+            bank = tr_psum.tile([P, 4, P], F32, tag="tr")
+            for s in range(4):
+                g, u = divmod(s, 2)
+                words = slice(2 * P * g + u, 2 * P * (g + 1), 2)
+                nc.tensor.transpose(bank[:, s, :], x_words[:, r, words], ident[:])
+            nc.scalar.copy(
+                out=x_grouped_words[:, :, r, :, :],
+                in_=bank[:].rearrange("p (g u) q -> p g q u", u=2),
+            )
+        x_codes = const.tile([P, PASSES0 * BATCH], U32, align_bytes=64)
+        x_scales = const.tile([P, PASSES0 * BATCH], U8, align_bytes=64)
+        nc.vector.quantize_mx(out=x_codes[:].bitcast(FP8X4), scales=x_scales[:], in_=x_grouped[:])
+
+        b0_words = b0_rows[:].bitcast(F32)
+        b0_bank = tr_psum.tile([P, BANK], F32, tag="tr")
+        for u in range(2):
+            nc.tensor.transpose(
+                b0_bank[:, P * u : P * (u + 1)], b0_words[:, u : 2 * P : 2], ident[:]
+            )
+        b0_cols = const.tile([P, D1 // P], F32)
+        b0_pairs = b0_bank[:, 0 : 2 * P].bitcast(BF16).rearrange("p (u g e) -> p u g e", u=2, e=2)
+        nc.vector.tensor_copy(
+            out=b0_cols[:].rearrange("p (g u e) -> p u g e", u=2, e=2),
+            in_=b0_pairs[:, :, 0:PASSES1, :],
+        )
+
+        b1_all = const.tile([P, D2], F32)
+        for i in range(D2 // BANK):
+            cols = slice(BANK * i, BANK * (i + 1))
+            b1_bank = acc_psum.tile([P, BANK], F32, tag="acc")
+            nc.tensor.matmul(b1_bank[:], lhsT=ones[:], rhs=b1_row[:, cols], start=True, stop=True)
+            nc.scalar.copy(out=b1_all[:, cols], in_=b1_bank[:])
+
+        h_codes = const.tile([P, PASSES1 * BATCH], U32, align_bytes=64)
+        h_scales = const.tile([P, PASSES1 * BATCH], U8, align_bytes=64)
+
+        for s in range(UNITS + LAG_FINISH1):
+            if s + AHEAD < UNITS:
+                load(s + AHEAD)
+            if 0 <= s - LAG_QUANTISE < UNITS:
+                quantise(s - LAG_QUANTISE)
+            if 0 <= s - LAG_TRANSPOSE < UNITS:
+                transpose(s - LAG_TRANSPOSE)
+            if 0 <= s - LAG_FINISH0 < UNITS0:
+                layer0_finish(s - LAG_FINISH0)
+            if 0 <= s - LAG_FINISH1 - UNITS0 < UNITS1:
+                layer1_finish(s - LAG_FINISH1 - UNITS0)
+            if 0 <= s - LAG_MATMUL0 < UNITS0:
+                layer0_matmuls(s - LAG_MATMUL0)
+            if 0 <= s - LAG_MATMUL1 - UNITS0 < UNITS1:
+                layer1_matmuls(s - LAG_MATMUL1 - UNITS0)
+            if s < UNITS:
+                multiply(s)

@@ -43,7 +43,8 @@ def tile_patchedsparsenetwork_pa_kernel(tc, x, W0, b0, m0, W1, b1, m1, out):
     with ExitStack() as ctx:
         ctx.enter_context(tc.manual_schedule())
         const = ctx.enter_context(tc.tile_pool(name="const", bufs=1))
-        weights = ctx.enter_context(tc.tile_pool(name="weights", bufs=AHEAD + LAG_TRANSPOSE + 1))
+        weights = ctx.enter_context(tc.tile_pool(name="weights", bufs=AHEAD + 1))
+        masked_pool = ctx.enter_context(tc.tile_pool(name="masked", bufs=LAG_TRANSPOSE + 2))
         grouped_pool = ctx.enter_context(
             tc.tile_pool(name="grouped", bufs=LAG_QUANTISE - LAG_TRANSPOSE + 2)
         )
@@ -54,7 +55,7 @@ def tile_patchedsparsenetwork_pa_kernel(tc, x, W0, b0, m0, W1, b1, m1, out):
         tr_psum = ctx.enter_context(tc.psum_pool(name="tr_psum", bufs=4))
         acc_psum = ctx.enter_context(tc.psum_pool(name="acc_psum", bufs=4))
 
-        w_of, m_of, grouped_of, codes_of, scales_of, acc_of = {}, {}, {}, {}, {}, {}
+        w_of, m_of, masked_of, grouped_of, codes_of, scales_of, acc_of = {}, {}, {}, {}, {}, {}, {}
         h_rows_of = {}
 
         def load(i):
@@ -74,10 +75,17 @@ def tile_patchedsparsenetwork_pa_kernel(tc, x, W0, b0, m0, W1, b1, m1, out):
             w_of[i], m_of[i] = w, m
 
         def multiply(i):
-            nc.vector.tensor_tensor(out=w_of[i][:], in0=w_of[i][:], in1=m_of[i][:], op=MULT)
+            masked = masked_pool.tile([P, UNIT], BF16, tag="masked")
+            nc.vector.tensor_tensor(
+                out=masked[:].rearrange("p (u w e) -> p u w e", u=2, e=2),
+                in0=w_of[i][:].rearrange("p (w u e) -> p u w e", u=2, e=2),
+                in1=m_of[i][:].rearrange("p (w u e) -> p u w e", u=2, e=2),
+                op=MULT,
+            )
+            masked_of[i] = masked
 
         def transpose(i):
-            w_words = w_of[i][:].bitcast(F32)
+            w_words = masked_of[i][:].bitcast(F32)
             grouped = grouped_pool.tile([P, UNIT], BF16, tag="grouped", align_bytes=64)
             grouped_words = grouped[:].bitcast(F32).rearrange(
                 "p (a c q u) -> p a c q u", a=2, c=2, u=2
@@ -86,8 +94,8 @@ def tile_patchedsparsenetwork_pa_kernel(tc, x, W0, b0, m0, W1, b1, m1, out):
                 bank = tr_psum.tile([P, 4, P], F32, tag="tr")
                 for s in range(4):
                     c, u = divmod(4 * a + s, 2)
-                    words = slice(2 * P * c + u, 2 * P * (c + 1), 2)
-                    nc.tensor.transpose(bank[:, s, :], w_words[:, words], ident[:])
+                    first = UNIT // 4 * u + P * c
+                    nc.tensor.transpose(bank[:, s, :], w_words[:, first : first + P], ident[:])
                 nc.scalar.copy(
                     out=grouped_words[:, a], in_=bank[:].rearrange("p (c u) q -> p c q u", u=2)
                 )

@@ -27,12 +27,12 @@ UNITS0 = D1 // ROWS0
 UNITS = UNITS0 + D2 // ROWS1
 UNITS1 = D2 // ROWS1
 
-LAG_TRANSPOSE = 1
-LAG_QUANTISE = 3
-LAG_MATMUL0 = 3
-LAG_FINISH0 = 5
-LAG_MATMUL1 = 4
-LAG_FINISH1 = 7
+LAG_QUANTISE0 = 1
+LAG_MATMUL0 = 1
+LAG_GROUP0 = 3
+LAG_QUANTISE1 = 2
+LAG_MATMUL1 = 3
+LAG_FINISH1 = 5
 AHEAD = 10
 
 FLOPS = 2 * BATCH * D0 * D1 + 2 * BATCH * D1 * D2
@@ -43,20 +43,19 @@ def tile_patchedsparsenetwork_pa_kernel(tc, x, W0, b0, m0, W1, b1, m1, out):
     with ExitStack() as ctx:
         ctx.enter_context(tc.manual_schedule())
         const = ctx.enter_context(tc.tile_pool(name="const", bufs=1))
-        weights = ctx.enter_context(tc.tile_pool(name="weights", bufs=AHEAD + 1))
-        masked_pool = ctx.enter_context(tc.tile_pool(name="masked", bufs=LAG_TRANSPOSE + 2))
-        grouped_pool = ctx.enter_context(
-            tc.tile_pool(name="grouped", bufs=LAG_QUANTISE - LAG_TRANSPOSE + 2)
-        )
+        weights = ctx.enter_context(tc.tile_pool(name="weights", bufs=AHEAD + 2))
+        sorted_pool = ctx.enter_context(tc.tile_pool(name="sorted", bufs=2))
+        grouped_pool = ctx.enter_context(tc.tile_pool(name="grouped", bufs=LAG_QUANTISE1 + 2))
         codes_pool = ctx.enter_context(
-            tc.tile_pool(name="codes", bufs=LAG_MATMUL1 - LAG_QUANTISE + 2)
+            tc.tile_pool(name="codes", bufs=LAG_MATMUL1 - LAG_QUANTISE1 + 2)
         )
+        turned_pool = ctx.enter_context(tc.tile_pool(name="turned", bufs=3))
         h_pool = ctx.enter_context(tc.tile_pool(name="h", bufs=2))
         tr_psum = ctx.enter_context(tc.psum_pool(name="tr_psum", bufs=4))
         acc_psum = ctx.enter_context(tc.psum_pool(name="acc_psum", bufs=4))
 
-        w_of, m_of, masked_of, grouped_of, codes_of, scales_of, acc_of = {}, {}, {}, {}, {}, {}, {}
-        h_rows_of = {}
+        w_of, m_of, product_of, grouped_of, codes_of, scales_of, acc_of = {}, {}, {}, {}, {}, {}, {}
+        h_rows_of, h_grouped_of, turned_of, back_of = {}, {}, {}, {}
 
         def load(i):
             w = weights.tile([P, UNIT], BF16, tag="w")
@@ -75,17 +74,21 @@ def tile_patchedsparsenetwork_pa_kernel(tc, x, W0, b0, m0, W1, b1, m1, out):
             w_of[i], m_of[i] = w, m
 
         def multiply(i):
-            masked = masked_pool.tile([P, UNIT], BF16, tag="masked")
+            if i < UNITS0:
+                product_of[i] = w_of[i]
+                nc.vector.tensor_tensor(out=w_of[i][:], in0=w_of[i][:], in1=m_of[i][:], op=MULT)
+                return
+            product = sorted_pool.tile([P, UNIT], BF16, tag="product")
+            product_of[i] = product
             nc.vector.tensor_tensor(
-                out=masked[:].rearrange("p (u w e) -> p u w e", u=2, e=2),
+                out=product[:].rearrange("p (u w e) -> p u w e", u=2, e=2),
                 in0=w_of[i][:].rearrange("p (w u e) -> p u w e", u=2, e=2),
                 in1=m_of[i][:].rearrange("p (w u e) -> p u w e", u=2, e=2),
                 op=MULT,
             )
-            masked_of[i] = masked
 
         def transpose(i):
-            w_words = masked_of[i][:].bitcast(F32)
+            w_words = product_of[i][:].bitcast(F32)
             grouped = grouped_pool.tile([P, UNIT], BF16, tag="grouped", align_bytes=64)
             grouped_words = grouped[:].bitcast(F32).rearrange(
                 "p (a c q u) -> p a c q u", a=2, c=2, u=2
@@ -94,8 +97,11 @@ def tile_patchedsparsenetwork_pa_kernel(tc, x, W0, b0, m0, W1, b1, m1, out):
                 bank = tr_psum.tile([P, 4, P], F32, tag="tr")
                 for s in range(4):
                     c, u = divmod(4 * a + s, 2)
-                    first = UNIT // 4 * u + P * c
-                    nc.tensor.transpose(bank[:, s, :], w_words[:, first : first + P], ident[:])
+                    if i < UNITS0:
+                        words = slice(2 * P * c + u, 2 * P * (c + 1), 2)
+                    else:
+                        words = slice(UNIT // 4 * u + P * c, UNIT // 4 * u + P * (c + 1))
+                    nc.tensor.transpose(bank[:, s, :], w_words[:, words], ident[:])
                 nc.scalar.copy(
                     out=grouped_words[:, a], in_=bank[:].rearrange("p (c u) q -> p c q u", u=2)
                 )
@@ -135,46 +141,94 @@ def tile_patchedsparsenetwork_pa_kernel(tc, x, W0, b0, m0, W1, b1, m1, out):
                     bias=b0_cols[:, 2 * j + e : 2 * j + e + 1],
                 )
 
-        def layer0_finish(j):
+        def layer0_group(j):
             g, u = divmod(j, 2)
             if u == 1:
                 h_grouped = h_pool.tile([P, BATCH, PACK], BF16, tag="h_grouped", align_bytes=64)
+                h_grouped_of[g] = h_grouped
                 nc.vector.tensor_copy(
                     out=h_grouped[:].rearrange("p (c i) t -> p c t i", i=4),
                     in_=h_rows_of[g][:].rearrange("p t (c i) -> p c t i", i=4),
                 )
+
+        def layer0_quantise(j):
+            g, u = divmod(j, 2)
+            if u == 1:
                 h_cols = slice(BATCH * g, BATCH * (g + 1))
                 nc.vector.quantize_mx(
                     out=h_codes[:, h_cols].bitcast(FP8X4),
                     scales=h_scales[:, h_cols],
-                    in_=h_grouped[:].rearrange("p n t -> p (n t)"),
+                    in_=h_grouped_of[g][:].rearrange("p n t -> p (n t)"),
                 )
 
+        def is_turned(k):
+            return k % 2 == 1 and k < UNITS1 - 1
+
         def layer1_matmuls(k):
-            acc = acc_psum.tile([P, BATCH_TILES, ROWS1], F32, tag="acc")
-            for r in range(BATCH_TILES):
+            codes, scales = codes_of[UNITS0 + k], scales_of[UNITS0 + k]
+            if is_turned(k):
+                acc = acc_psum.tile([P, BATCH], F32, tag="acc")
                 for g in range(PASSES1):
-                    h_cols = slice(BATCH * g + P * r, BATCH * g + P * (r + 1))
+                    h_cols = slice(BATCH * g, BATCH * (g + 1))
                     w_cols = slice(ROWS1 * g, ROWS1 * (g + 1))
                     nc.tensor.matmul_mx(
-                        out=acc[:, r, :],
-                        lhsT=h_codes[:, h_cols].bitcast(FP8X4),
-                        lhsT_scale=h_scales[:, h_cols],
-                        rhs=codes_of[UNITS0 + k][:, w_cols].bitcast(FP8X4),
-                        rhs_scale=scales_of[UNITS0 + k][:, w_cols],
+                        out=acc[:],
+                        lhsT=codes[:, w_cols].bitcast(FP8X4),
+                        lhsT_scale=scales[:, w_cols],
+                        rhs=h_codes[:, h_cols].bitcast(FP8X4),
+                        rhs_scale=h_scales[:, h_cols],
                         start=(g == 0),
                         stop=(g == PASSES1 - 1),
                     )
+            else:
+                acc = acc_psum.tile([P, BATCH_TILES, ROWS1], F32, tag="acc")
+                for r in range(BATCH_TILES):
+                    for g in range(PASSES1):
+                        h_cols = slice(BATCH * g + P * r, BATCH * g + P * (r + 1))
+                        w_cols = slice(ROWS1 * g, ROWS1 * (g + 1))
+                        nc.tensor.matmul_mx(
+                            out=acc[:, r, :],
+                            lhsT=h_codes[:, h_cols].bitcast(FP8X4),
+                            lhsT_scale=h_scales[:, h_cols],
+                            rhs=codes[:, w_cols].bitcast(FP8X4),
+                            rhs_scale=scales[:, w_cols],
+                            start=(g == 0),
+                            stop=(g == PASSES1 - 1),
+                        )
             acc_of[k] = acc
 
-        def layer1_finish(k):
-            part = out_rows[:, :, ROWS1 * k : ROWS1 * (k + 1)]
+        def turned_relu(k):
+            turned = turned_pool.tile([P, BATCH], F32, tag="turned")
+            turned_of[k] = turned
+            nc.scalar.activation(
+                out=turned[:], in_=acc_of[k][:], func=RELU, bias=b1_cols[:, k : k + 1]
+            )
+
+        def turn_back(k):
+            bank = tr_psum.tile([P, BATCH_TILES, P], F32, tag="tr")
+            back_of[k] = bank
+            for r in range(BATCH_TILES):
+                nc.tensor.transpose(bank[:, r, :], turned_of[k][:, P * r : P * (r + 1)], ident[:])
+
+        def add(k):
             bias = b1_all[:, ROWS1 * k : ROWS1 * (k + 1)].unsqueeze(1)
             nc.vector.tensor_tensor(
-                out=part, in0=acc_of[k][:], in1=bias.to_broadcast([P, BATCH_TILES, ROWS1]), op=ADD
+                out=out_rows[:, :, ROWS1 * k : ROWS1 * (k + 1)],
+                in0=acc_of[k][:],
+                in1=bias.to_broadcast([P, BATCH_TILES, ROWS1]),
+                op=ADD,
             )
-            nc.scalar.activation(out=part, in_=part, func=RELU)
-            nc.sync.dma_start(out=out_view[:, :, ROWS1 * k : ROWS1 * (k + 1)], in_=part)
+
+        def finish(k):
+            part = out_rows[:, :, ROWS1 * k : ROWS1 * (k + 1)]
+            if is_turned(k):
+                nc.scalar.copy(out=part, in_=back_of[k][:])
+            else:
+                nc.scalar.activation(out=part, in_=part, func=RELU)
+            if k >= UNITS1 - 2 or k % 2 == 1:
+                first = k if k >= UNITS1 - 2 else k - 1
+                cols = slice(ROWS1 * first, ROWS1 * (k + 1))
+                nc.sync.dma_start(out=out_view[:, :, cols], in_=out_rows[:, :, cols])
 
         x_rows = const.tile([P, BATCH_TILES * D0], BF16)
         nc.sync.dma_start(out=x_rows[:], in_=x.rearrange("(q r) k -> q (r k)", r=BATCH_TILES))
@@ -182,18 +236,24 @@ def tile_patchedsparsenetwork_pa_kernel(tc, x, W0, b0, m0, W1, b1, m1, out):
         out_rows = const.tile([P, BATCH_TILES, D2], F32)
 
         b0_rows = const.tile([P, K_PASS], BF16)
+        b1_rows = const.tile([P, P], BF16)
         b1_row = const.tile([P, D2], BF16)
         ones = const.tile([P, P], BF16)
         nc.vector.memset(b0_rows[:], 0.0)
+        nc.vector.memset(b1_rows[:], 0.0)
         nc.vector.memset(b1_row[:], 0.0)
         nc.vector.memset(ones[:], 1.0)
         nc.sync.dma_start(out=b0_rows[0:PASSES1, :], in_=b0.rearrange("(g c) -> g c", c=K_PASS))
+        nc.sync.dma_start(out=b1_rows[0:UNITS1, :], in_=b1.rearrange("(k c) -> k c", c=ROWS1))
         nc.sync.dma_start(out=b1_row[0:1, :], in_=b1.rearrange("(o d) -> o d", o=1))
         for i in range(AHEAD):
             load(i)
 
         ident = const.tile([P, P], F32)
         make_identity(nc, ident[:])
+        ident_bf16 = const.tile([P, P], BF16)
+        make_identity(nc, ident_bf16[:])
+        multiply(0)
 
         x_words = x_rows[:].bitcast(F32).rearrange("q (r w) -> q r w", r=BATCH_TILES)
         x_grouped = const.tile([P, PASSES0 * BATCH * PACK], BF16, align_bytes=64)
@@ -227,6 +287,13 @@ def tile_patchedsparsenetwork_pa_kernel(tc, x, W0, b0, m0, W1, b1, m1, out):
             in_=b0_pairs[:, :, 0:PASSES1, :],
         )
 
+        b1_bank = acc_psum.tile([P, BANK], F32, tag="acc")
+        nc.tensor.matmul(
+            b1_bank[:, 0:P], lhsT=b1_rows[:], rhs=ident_bf16[:], start=True, stop=True
+        )
+        b1_cols = const.tile([P, UNITS1], F32)
+        nc.vector.tensor_copy(out=b1_cols[:], in_=b1_bank[:, 0:UNITS1])
+
         b1_all = const.tile([P, D2], F32)
         for i in range(D2 // BANK):
             cols = slice(BANK * i, BANK * (i + 1))
@@ -238,19 +305,31 @@ def tile_patchedsparsenetwork_pa_kernel(tc, x, W0, b0, m0, W1, b1, m1, out):
         h_scales = const.tile([P, PASSES1 * BATCH], U8, align_bytes=64)
 
         for s in range(UNITS + LAG_FINISH1):
+            k_mx = s - LAG_MATMUL1 - UNITS0
+            k_out = s - LAG_FINISH1 - UNITS0
             if s + AHEAD < UNITS:
                 load(s + AHEAD)
-            if 0 <= s - LAG_QUANTISE < UNITS:
-                quantise(s - LAG_QUANTISE)
-            if 0 <= s - LAG_TRANSPOSE < UNITS:
-                transpose(s - LAG_TRANSPOSE)
-            if 0 <= s - LAG_FINISH0 < UNITS0:
-                layer0_finish(s - LAG_FINISH0)
-            if 0 <= s - LAG_FINISH1 - UNITS0 < UNITS1:
-                layer1_finish(s - LAG_FINISH1 - UNITS0)
+            if 0 < s < UNITS:
+                multiply(s)
+            if s < UNITS:
+                transpose(s)
+            if 0 <= k_out and is_turned(k_out):
+                turn_back(k_out)
+            if 0 <= s - LAG_GROUP0 < UNITS0:
+                layer0_group(s - LAG_GROUP0)
+            if 0 <= s - LAG_QUANTISE0 < UNITS0:
+                quantise(s - LAG_QUANTISE0)
+            if UNITS0 <= s - LAG_QUANTISE1 < UNITS:
+                quantise(s - LAG_QUANTISE1)
+            if 0 <= s - LAG_GROUP0 < UNITS0:
+                layer0_quantise(s - LAG_GROUP0)
+            if 0 <= k_out:
+                if not is_turned(k_out):
+                    add(k_out)
+                finish(k_out)
             if 0 <= s - LAG_MATMUL0 < UNITS0:
                 layer0_matmuls(s - LAG_MATMUL0)
-            if 0 <= s - LAG_MATMUL1 - UNITS0 < UNITS1:
-                layer1_matmuls(s - LAG_MATMUL1 - UNITS0)
-            if s < UNITS:
-                multiply(s)
+            if 0 <= k_mx < UNITS1:
+                layer1_matmuls(k_mx)
+                if is_turned(k_mx):
+                    turned_relu(k_mx)

@@ -31,8 +31,9 @@ LAG_QUANTISE0 = 1
 LAG_MATMUL0 = 1
 LAG_GROUP0 = 3
 LAG_QUANTISE1 = 2
-LAG_MATMUL1 = 3
-LAG_FINISH1 = 5
+LAG_MATMUL1 = 2
+LAG_FINISH1 = 4
+FIRST_SORTED = UNITS0 + 3
 AHEAD = 10
 
 FLOPS = 2 * BATCH * D0 * D1 + 2 * BATCH * D1 * D2
@@ -74,7 +75,7 @@ def tile_patchedsparsenetwork_pa_kernel(tc, x, W0, b0, m0, W1, b1, m1, out):
             w_of[i], m_of[i] = w, m
 
         def multiply(i):
-            if i < UNITS0:
+            if i < FIRST_SORTED:
                 product_of[i] = w_of[i]
                 nc.vector.tensor_tensor(out=w_of[i][:], in0=w_of[i][:], in1=m_of[i][:], op=MULT)
                 return
@@ -97,7 +98,7 @@ def tile_patchedsparsenetwork_pa_kernel(tc, x, W0, b0, m0, W1, b1, m1, out):
                 bank = tr_psum.tile([P, 4, P], F32, tag="tr")
                 for s in range(4):
                     c, u = divmod(4 * a + s, 2)
-                    if i < UNITS0:
+                    if i < FIRST_SORTED:
                         words = slice(2 * P * c + u, 2 * P * (c + 1), 2)
                     else:
                         words = slice(UNIT // 4 * u + P * c, UNIT // 4 * u + P * (c + 1))
@@ -162,7 +163,7 @@ def tile_patchedsparsenetwork_pa_kernel(tc, x, W0, b0, m0, W1, b1, m1, out):
                 )
 
         def is_turned(k):
-            return k % 2 == 1 and k < UNITS1 - 1
+            return k % 2 == 0 and k < UNITS1 - 2
 
         def layer1_matmuls(k):
             codes, scales = codes_of[UNITS0 + k], scales_of[UNITS0 + k]
@@ -225,8 +226,8 @@ def tile_patchedsparsenetwork_pa_kernel(tc, x, W0, b0, m0, W1, b1, m1, out):
                 nc.scalar.copy(out=part, in_=back_of[k][:])
             else:
                 nc.scalar.activation(out=part, in_=part, func=RELU)
-            if k >= UNITS1 - 2 or k % 2 == 1:
-                first = k if k >= UNITS1 - 2 else k - 1
+            if k >= UNITS1 - 4 or k % 2 == 1:
+                first = k if k >= UNITS1 - 4 else k - 1
                 cols = slice(ROWS1 * first, ROWS1 * (k + 1))
                 nc.sync.dma_start(out=out_view[:, :, cols], in_=out_rows[:, :, cols])
 
@@ -237,15 +238,10 @@ def tile_patchedsparsenetwork_pa_kernel(tc, x, W0, b0, m0, W1, b1, m1, out):
 
         b0_rows = const.tile([P, K_PASS], BF16)
         b1_rows = const.tile([P, P], BF16)
-        b1_row = const.tile([P, D2], BF16)
-        ones = const.tile([P, P], BF16)
         nc.vector.memset(b0_rows[:], 0.0)
         nc.vector.memset(b1_rows[:], 0.0)
-        nc.vector.memset(b1_row[:], 0.0)
-        nc.vector.memset(ones[:], 1.0)
         nc.sync.dma_start(out=b0_rows[0:PASSES1, :], in_=b0.rearrange("(g c) -> g c", c=K_PASS))
         nc.sync.dma_start(out=b1_rows[0:UNITS1, :], in_=b1.rearrange("(k c) -> k c", c=ROWS1))
-        nc.sync.dma_start(out=b1_row[0:1, :], in_=b1.rearrange("(o d) -> o d", o=1))
         for i in range(AHEAD):
             load(i)
 
@@ -272,7 +268,6 @@ def tile_patchedsparsenetwork_pa_kernel(tc, x, W0, b0, m0, W1, b1, m1, out):
             )
         x_codes = const.tile([P, PASSES0 * BATCH], U32, align_bytes=64)
         x_scales = const.tile([P, PASSES0 * BATCH], U8, align_bytes=64)
-        nc.vector.quantize_mx(out=x_codes[:].bitcast(FP8X4), scales=x_scales[:], in_=x_grouped[:])
 
         b0_words = b0_rows[:].bitcast(F32)
         b0_bank = tr_psum.tile([P, BANK], F32, tag="tr")
@@ -295,11 +290,45 @@ def tile_patchedsparsenetwork_pa_kernel(tc, x, W0, b0, m0, W1, b1, m1, out):
         nc.vector.tensor_copy(out=b1_cols[:], in_=b1_bank[:, 0:UNITS1])
 
         b1_all = const.tile([P, D2], F32)
-        for i in range(D2 // BANK):
-            cols = slice(BANK * i, BANK * (i + 1))
-            b1_bank = acc_psum.tile([P, BANK], F32, tag="acc")
-            nc.tensor.matmul(b1_bank[:], lhsT=ones[:], rhs=b1_row[:, cols], start=True, stop=True)
-            nc.scalar.copy(out=b1_all[:, cols], in_=b1_bank[:])
+
+        def last_unit():
+            k = UNITS1 - 1
+            codes, scales = codes_of[UNITS0 + k], scales_of[UNITS0 + k]
+            cols = slice(ROWS1 * k, ROWS1 * (k + 1))
+            half = BATCH_TILES // 2
+            bias = b1_all[:, cols].unsqueeze(1).to_broadcast([P, half, ROWS1])
+            for tiles in (slice(0, half), slice(half, BATCH_TILES)):
+                acc = acc_psum.tile([P, half, ROWS1], F32, tag="acc")
+                for r in range(tiles.start, tiles.stop):
+                    for g in range(PASSES1):
+                        h_cols = slice(BATCH * g + P * r, BATCH * g + P * (r + 1))
+                        w_cols = slice(ROWS1 * g, ROWS1 * (g + 1))
+                        nc.tensor.matmul_mx(
+                            out=acc[:, r - tiles.start, :],
+                            lhsT=h_codes[:, h_cols].bitcast(FP8X4),
+                            lhsT_scale=h_scales[:, h_cols],
+                            rhs=codes[:, w_cols].bitcast(FP8X4),
+                            rhs_scale=scales[:, w_cols],
+                            start=(g == 0),
+                            stop=(g == PASSES1 - 1),
+                        )
+                part = out_rows[:, tiles, cols]
+                nc.vector.tensor_tensor(out=part, in0=acc[:], in1=bias, op=ADD)
+                nc.scalar.activation(out=part, in_=part, func=RELU)
+                nc.sync.dma_start(out=out_view[:, tiles, cols], in_=part)
+
+        def spread_b1(k):
+            b1_bank = tr_psum.tile([P, BANK], F32, tag="tr")
+            nc.tensor.matmul(
+                b1_bank[:, 0:ROWS1],
+                lhsT=ident_bf16[:, k : k + 1].to_broadcast([P, P]),
+                rhs=b1_rows[:],
+                start=True,
+                stop=True,
+            )
+            nc.scalar.copy(
+                out=b1_all[:, ROWS1 * k : ROWS1 * (k + 1)], in_=b1_bank[:, 0:ROWS1]
+            )
 
         h_codes = const.tile([P, PASSES1 * BATCH], U32, align_bytes=64)
         h_scales = const.tile([P, PASSES1 * BATCH], U8, align_bytes=64)
@@ -313,7 +342,11 @@ def tile_patchedsparsenetwork_pa_kernel(tc, x, W0, b0, m0, W1, b1, m1, out):
                 multiply(s)
             if s < UNITS:
                 transpose(s)
-            if 0 <= k_out and is_turned(k_out):
+            if s == 1:
+                nc.vector.quantize_mx(
+                    out=x_codes[:].bitcast(FP8X4), scales=x_scales[:], in_=x_grouped[:]
+                )
+            if 0 <= k_out < UNITS1 and is_turned(k_out):
                 turn_back(k_out)
             if 0 <= s - LAG_GROUP0 < UNITS0:
                 layer0_group(s - LAG_GROUP0)
@@ -321,15 +354,19 @@ def tile_patchedsparsenetwork_pa_kernel(tc, x, W0, b0, m0, W1, b1, m1, out):
                 quantise(s - LAG_QUANTISE0)
             if UNITS0 <= s - LAG_QUANTISE1 < UNITS:
                 quantise(s - LAG_QUANTISE1)
+            if UNITS0 <= s - 1 < UNITS and not is_turned(s - 1 - UNITS0):
+                spread_b1(s - 1 - UNITS0)
             if 0 <= s - LAG_GROUP0 < UNITS0:
                 layer0_quantise(s - LAG_GROUP0)
-            if 0 <= k_out:
+            if 0 <= k_out < UNITS1 - 1:
                 if not is_turned(k_out):
                     add(k_out)
                 finish(k_out)
             if 0 <= s - LAG_MATMUL0 < UNITS0:
                 layer0_matmuls(s - LAG_MATMUL0)
-            if 0 <= k_mx < UNITS1:
+            if 0 <= k_mx < UNITS1 - 1:
                 layer1_matmuls(k_mx)
                 if is_turned(k_mx):
                     turned_relu(k_mx)
+            if s == UNITS + LAG_FINISH1 - 2:
+                last_unit()

@@ -33,7 +33,8 @@ LAG_GROUP0 = 3
 LAG_QUANTISE1 = 2
 LAG_MATMUL1 = 2
 LAG_FINISH1 = 4
-FIRST_SORTED = UNITS0 + 3
+FIRST_SORTED = UNITS0 + 4
+STORE_ENDS = (0, 4, 8, 10, 11, 12, 13, 14, 15)
 AHEAD = 10
 
 FLOPS = 2 * BATCH * D0 * D1 + 2 * BATCH * D1 * D2
@@ -48,7 +49,7 @@ def tile_patchedsparsenetwork_pa_kernel(tc, x, W0, b0, m0, W1, b1, m1, out):
         sorted_pool = ctx.enter_context(tc.tile_pool(name="sorted", bufs=2))
         grouped_pool = ctx.enter_context(tc.tile_pool(name="grouped", bufs=LAG_QUANTISE1 + 2))
         codes_pool = ctx.enter_context(
-            tc.tile_pool(name="codes", bufs=LAG_MATMUL1 - LAG_QUANTISE1 + 2)
+            tc.tile_pool(name="codes", bufs=LAG_MATMUL1 - LAG_QUANTISE1 + 3)
         )
         turned_pool = ctx.enter_context(tc.tile_pool(name="turned", bufs=3))
         h_pool = ctx.enter_context(tc.tile_pool(name="h", bufs=2))
@@ -163,7 +164,7 @@ def tile_patchedsparsenetwork_pa_kernel(tc, x, W0, b0, m0, W1, b1, m1, out):
                 )
 
         def is_turned(k):
-            return k % 2 == 0 and k < UNITS1 - 2
+            return k % 2 == 0 and k < UNITS1 - 4
 
         def layer1_matmuls(k):
             codes, scales = codes_of[UNITS0 + k], scales_of[UNITS0 + k]
@@ -226,8 +227,8 @@ def tile_patchedsparsenetwork_pa_kernel(tc, x, W0, b0, m0, W1, b1, m1, out):
                 nc.scalar.copy(out=part, in_=back_of[k][:])
             else:
                 nc.scalar.activation(out=part, in_=part, func=RELU)
-            if k >= UNITS1 - 4 or k % 2 == 1:
-                first = k if k >= UNITS1 - 4 else k - 1
+            if k + 1 in STORE_ENDS:
+                first = max(end for end in STORE_ENDS if end <= k)
                 cols = slice(ROWS1 * first, ROWS1 * (k + 1))
                 nc.sync.dma_start(out=out_view[:, :, cols], in_=out_rows[:, :, cols])
 
@@ -240,10 +241,11 @@ def tile_patchedsparsenetwork_pa_kernel(tc, x, W0, b0, m0, W1, b1, m1, out):
         b1_rows = const.tile([P, P], BF16)
         nc.vector.memset(b0_rows[:], 0.0)
         nc.vector.memset(b1_rows[:], 0.0)
-        nc.sync.dma_start(out=b0_rows[0:PASSES1, :], in_=b0.rearrange("(g c) -> g c", c=K_PASS))
-        nc.sync.dma_start(out=b1_rows[0:UNITS1, :], in_=b1.rearrange("(k c) -> k c", c=ROWS1))
         for i in range(AHEAD):
             load(i)
+            if i == 1:
+                nc.sync.dma_start(out=b0_rows[0:PASSES1, :], in_=b0.rearrange("(g c) -> g c", c=K_PASS))
+                nc.sync.dma_start(out=b1_rows[0:UNITS1, :], in_=b1.rearrange("(k c) -> k c", c=ROWS1))
 
         ident = const.tile([P, P], F32)
         make_identity(nc, ident[:])
@@ -269,25 +271,27 @@ def tile_patchedsparsenetwork_pa_kernel(tc, x, W0, b0, m0, W1, b1, m1, out):
         x_codes = const.tile([P, PASSES0 * BATCH], U32, align_bytes=64)
         x_scales = const.tile([P, PASSES0 * BATCH], U8, align_bytes=64)
 
-        b0_words = b0_rows[:].bitcast(F32)
-        b0_bank = tr_psum.tile([P, BANK], F32, tag="tr")
-        for u in range(2):
-            nc.tensor.transpose(
-                b0_bank[:, P * u : P * (u + 1)], b0_words[:, u : 2 * P : 2], ident[:]
-            )
         b0_cols = const.tile([P, D1 // P], F32)
-        b0_pairs = b0_bank[:, 0 : 2 * P].bitcast(BF16).rearrange("p (u g e) -> p u g e", u=2, e=2)
-        nc.vector.tensor_copy(
-            out=b0_cols[:].rearrange("p (g u e) -> p u g e", u=2, e=2),
-            in_=b0_pairs[:, :, 0:PASSES1, :],
-        )
-
-        b1_bank = acc_psum.tile([P, BANK], F32, tag="acc")
-        nc.tensor.matmul(
-            b1_bank[:, 0:P], lhsT=b1_rows[:], rhs=ident_bf16[:], start=True, stop=True
-        )
         b1_cols = const.tile([P, UNITS1], F32)
-        nc.vector.tensor_copy(out=b1_cols[:], in_=b1_bank[:, 0:UNITS1])
+
+        def bias_columns():
+            b0_words = b0_rows[:].bitcast(F32)
+            b0_bank = tr_psum.tile([P, BANK], F32, tag="tr")
+            for u in range(2):
+                nc.tensor.transpose(
+                    b0_bank[:, P * u : P * (u + 1)], b0_words[:, u : 2 * P : 2], ident[:]
+                )
+            b0_pairs = b0_bank[:, 0 : 2 * P].bitcast(BF16).rearrange("p (u g e) -> p u g e", u=2, e=2)
+            nc.vector.tensor_copy(
+                out=b0_cols[:].rearrange("p (g u e) -> p u g e", u=2, e=2),
+                in_=b0_pairs[:, :, 0:PASSES1, :],
+            )
+
+            b1_bank = acc_psum.tile([P, BANK], F32, tag="acc")
+            nc.tensor.matmul(
+                b1_bank[:, 0:P], lhsT=b1_rows[:], rhs=ident_bf16[:], start=True, stop=True
+            )
+            nc.vector.tensor_copy(out=b1_cols[:], in_=b1_bank[:, 0:UNITS1])
 
         b1_all = const.tile([P, D2], F32)
 
@@ -338,6 +342,10 @@ def tile_patchedsparsenetwork_pa_kernel(tc, x, W0, b0, m0, W1, b1, m1, out):
             k_out = s - LAG_FINISH1 - UNITS0
             if s + AHEAD < UNITS:
                 load(s + AHEAD)
+            if 0 <= k_out < UNITS1 and is_turned(k_out):
+                turn_back(k_out)
+            if 0 <= k_out < UNITS1 - 1 and is_turned(k_out):
+                finish(k_out)
             if 0 < s < UNITS:
                 multiply(s)
             if s < UNITS:
@@ -346,21 +354,20 @@ def tile_patchedsparsenetwork_pa_kernel(tc, x, W0, b0, m0, W1, b1, m1, out):
                 nc.vector.quantize_mx(
                     out=x_codes[:].bitcast(FP8X4), scales=x_scales[:], in_=x_grouped[:]
                 )
-            if 0 <= k_out < UNITS1 and is_turned(k_out):
-                turn_back(k_out)
             if 0 <= s - LAG_GROUP0 < UNITS0:
                 layer0_group(s - LAG_GROUP0)
             if 0 <= s - LAG_QUANTISE0 < UNITS0:
                 quantise(s - LAG_QUANTISE0)
+            if s == 1:
+                bias_columns()
             if UNITS0 <= s - LAG_QUANTISE1 < UNITS:
                 quantise(s - LAG_QUANTISE1)
             if UNITS0 <= s - 1 < UNITS and not is_turned(s - 1 - UNITS0):
                 spread_b1(s - 1 - UNITS0)
             if 0 <= s - LAG_GROUP0 < UNITS0:
                 layer0_quantise(s - LAG_GROUP0)
-            if 0 <= k_out < UNITS1 - 1:
-                if not is_turned(k_out):
-                    add(k_out)
+            if 0 <= k_out < UNITS1 - 1 and not is_turned(k_out):
+                add(k_out)
                 finish(k_out)
             if 0 <= s - LAG_MATMUL0 < UNITS0:
                 layer0_matmuls(s - LAG_MATMUL0)

from contextlib import ExitStack

import concourse.mybir as mybir
from concourse.masks import make_identity

F32 = mybir.dt.float32
BF16 = mybir.dt.bfloat16
U32 = mybir.dt.uint32
U8 = mybir.dt.uint8
FP8X4 = mybir.dt.float8_e4m3fn_x4
MULT = mybir.AluOpType.mult
ADD = mybir.AluOpType.add
RELU = mybir.ActivationFunctionType.Relu

P = 128
PACK = 4
K_PASS = P * PACK
BANK = 512
BATCH, D0, D1, D2 = 512, 1024, 2048, 2048
PASSES0 = D0 // K_PASS
PASSES1 = D1 // K_PASS
BATCH_TILES = BATCH // P
UNIT = 2048
ROWS0 = P * UNIT // D0
ROWS1 = P * UNIT // D1
UNITS0 = D1 // ROWS0
UNITS = UNITS0 + D2 // ROWS1
UNITS1 = D2 // ROWS1

LAG_QUANTISE0 = 1
LAG_MATMUL0 = 1
LAG_GROUP0 = 3
LAG_QUANTISE1 = 2
LAG_MATMUL1 = 2
LAG_FINISH1 = 4
FIRST_SORTED = UNITS0 + 4
STORE_ENDS = (0, 4, 8, 10, 11, 12, 13, 14, 15)
AHEAD = 10

FLOPS = 2 * BATCH * D0 * D1 + 2 * BATCH * D1 * D2


def tile_patchedsparsenetwork_pa_kernel(tc, x, W0, b0, m0, W1, b1, m1, out):
    nc = tc.nc
    with ExitStack() as ctx:
        ctx.enter_context(tc.manual_schedule())
        const = ctx.enter_context(tc.tile_pool(name="const", bufs=1))
        weights = ctx.enter_context(tc.tile_pool(name="weights", bufs=AHEAD + 2))
        sorted_pool = ctx.enter_context(tc.tile_pool(name="sorted", bufs=2))
        grouped_pool = ctx.enter_context(tc.tile_pool(name="grouped", bufs=LAG_QUANTISE1 + 2))
        codes_pool = ctx.enter_context(
            tc.tile_pool(name="codes", bufs=LAG_MATMUL1 - LAG_QUANTISE1 + 3)
        )
        turned_pool = ctx.enter_context(tc.tile_pool(name="turned", bufs=3))
        h_pool = ctx.enter_context(tc.tile_pool(name="h", bufs=2))
        tr_psum = ctx.enter_context(tc.psum_pool(name="tr_psum", bufs=4))
        acc_psum = ctx.enter_context(tc.psum_pool(name="acc_psum", bufs=4))

        w_of, m_of, product_of, grouped_of, codes_of, scales_of, acc_of = {}, {}, {}, {}, {}, {}, {}
        h_rows_of, h_grouped_of, turned_of, back_of = {}, {}, {}, {}

        def load(i):
            w = weights.tile([P, UNIT], BF16, tag="w")
            m = weights.tile([P, UNIT], BF16, tag="m")
            if i < UNITS0:
                g, u = divmod(i, 2)
                rows = slice(K_PASS * g, K_PASS * (g + 1))
                w_rows = W0[rows, :].rearrange("(q u e) k -> u q (e k)", u=2, e=2)
                m_rows = m0[rows, :].rearrange("(q u e) k -> u q (e k)", u=2, e=2)
                nc.sync.dma_start(out=w[:], in_=w_rows[u])
                nc.sync.dma_start(out=m[:], in_=m_rows[u])
            else:
                rows = slice(ROWS1 * (i - UNITS0), ROWS1 * (i - UNITS0 + 1))
                nc.sync.dma_start(out=w[:], in_=W1[rows, :])
                nc.sync.dma_start(out=m[:], in_=m1[rows, :])
            w_of[i], m_of[i] = w, m

        def multiply(i):
            if i < FIRST_SORTED:
                product_of[i] = w_of[i]
                nc.vector.tensor_tensor(out=w_of[i][:], in0=w_of[i][:], in1=m_of[i][:], op=MULT)
                return
            product = sorted_pool.tile([P, UNIT], BF16, tag="product")
            product_of[i] = product
            nc.vector.tensor_tensor(
                out=product[:].rearrange("p (u w e) -> p u w e", u=2, e=2),
                in0=w_of[i][:].rearrange("p (w u e) -> p u w e", u=2, e=2),
                in1=m_of[i][:].rearrange("p (w u e) -> p u w e", u=2, e=2),
                op=MULT,
            )

        def transpose(i):
            w_words = product_of[i][:].bitcast(F32)
            grouped = grouped_pool.tile([P, UNIT], BF16, tag="grouped", align_bytes=64)
            grouped_words = grouped[:].bitcast(F32).rearrange(
                "p (a c q u) -> p a c q u", a=2, c=2, u=2
            )
            for a in range(2):
                bank = tr_psum.tile([P, 4, P], F32, tag="tr")
                for s in range(4):
                    c, u = divmod(4 * a + s, 2)
                    if i < FIRST_SORTED:
                        words = slice(2 * P * c + u, 2 * P * (c + 1), 2)
                    else:
                        words = slice(UNIT // 4 * u + P * c, UNIT // 4 * u + P * (c + 1))
                    nc.tensor.transpose(bank[:, s, :], w_words[:, words], ident[:])
                nc.scalar.copy(
                    out=grouped_words[:, a], in_=bank[:].rearrange("p (c u) q -> p c q u", u=2)
                )
            grouped_of[i] = grouped

        def quantise(i):
            codes = codes_pool.tile([P, UNIT // PACK], U32, tag="codes", align_bytes=64)
            scales = codes_pool.tile([P, UNIT // PACK], U8, tag="scales", align_bytes=64)
            nc.vector.quantize_mx(
                out=codes[:].bitcast(FP8X4), scales=scales[:], in_=grouped_of[i][:]
            )
            codes_of[i], scales_of[i] = codes, scales

        def layer0_matmuls(j):
            g, u = divmod(j, 2)
            if u == 0:
                h_rows = h_pool.tile([P, PACK, BATCH], BF16, tag="h_rows")
                h_rows_of[g] = h_rows
            for e in range(2):
                acc = acc_psum.tile([P, BATCH], F32, tag="acc")
                for g0 in range(PASSES0):
                    w_cols = slice(P * (PASSES0 * e + g0), P * (PASSES0 * e + g0 + 1))
                    x_cols = slice(BATCH * g0, BATCH * (g0 + 1))
                    nc.tensor.matmul_mx(
                        out=acc[:],
                        lhsT=codes_of[j][:, w_cols].bitcast(FP8X4),
                        lhsT_scale=scales_of[j][:, w_cols],
                        rhs=x_codes[:, x_cols].bitcast(FP8X4),
                        rhs_scale=x_scales[:, x_cols],
                        start=(g0 == 0),
                        stop=(g0 == PASSES0 - 1),
                    )
                nc.scalar.activation(
                    out=h_rows_of[g][:, 2 * u + e, :],
                    in_=acc[:],
                    func=RELU,
                    bias=b0_cols[:, 2 * j + e : 2 * j + e + 1],
                )

        def layer0_group(j):
            g, u = divmod(j, 2)
            if u == 1:
                h_grouped = h_pool.tile([P, BATCH, PACK], BF16, tag="h_grouped", align_bytes=64)
                h_grouped_of[g] = h_grouped
                nc.vector.tensor_copy(
                    out=h_grouped[:].rearrange("p (c i) t -> p c t i", i=4),
                    in_=h_rows_of[g][:].rearrange("p t (c i) -> p c t i", i=4),
                )

        def layer0_quantise(j):
            g, u = divmod(j, 2)
            if u == 1:
                h_cols = slice(BATCH * g, BATCH * (g + 1))
                nc.vector.quantize_mx(
                    out=h_codes[:, h_cols].bitcast(FP8X4),
                    scales=h_scales[:, h_cols],
                    in_=h_grouped_of[g][:].rearrange("p n t -> p (n t)"),
                )

        def is_turned(k):
            return k % 2 == 0 and k < UNITS1 - 4

        def layer1_matmuls(k):
            codes, scales = codes_of[UNITS0 + k], scales_of[UNITS0 + k]
            if is_turned(k):
                acc = acc_psum.tile([P, BATCH], F32, tag="acc")
                for g in range(PASSES1):
                    h_cols = slice(BATCH * g, BATCH * (g + 1))
                    w_cols = slice(ROWS1 * g, ROWS1 * (g + 1))
                    nc.tensor.matmul_mx(
                        out=acc[:],
                        lhsT=codes[:, w_cols].bitcast(FP8X4),
                        lhsT_scale=scales[:, w_cols],
                        rhs=h_codes[:, h_cols].bitcast(FP8X4),
                        rhs_scale=h_scales[:, h_cols],
                        start=(g == 0),
                        stop=(g == PASSES1 - 1),
                    )
            else:
                acc = acc_psum.tile([P, BATCH_TILES, ROWS1], F32, tag="acc")
                for r in range(BATCH_TILES):
                    for g in range(PASSES1):
                        h_cols = slice(BATCH * g + P * r, BATCH * g + P * (r + 1))
                        w_cols = slice(ROWS1 * g, ROWS1 * (g + 1))
                        nc.tensor.matmul_mx(
                            out=acc[:, r, :],
                            lhsT=h_codes[:, h_cols].bitcast(FP8X4),
                            lhsT_scale=h_scales[:, h_cols],
                            rhs=codes[:, w_cols].bitcast(FP8X4),
                            rhs_scale=scales[:, w_cols],
                            start=(g == 0),
                            stop=(g == PASSES1 - 1),
                        )
            acc_of[k] = acc

        def turned_relu(k):
            turned = turned_pool.tile([P, BATCH], F32, tag="turned")
            turned_of[k] = turned
            nc.scalar.activation(
                out=turned[:], in_=acc_of[k][:], func=RELU, bias=b1_cols[:, k : k + 1]
            )

        def turn_back(k):
            bank = tr_psum.tile([P, BATCH_TILES, P], F32, tag="tr")
            back_of[k] = bank
            for r in range(BATCH_TILES):
                nc.tensor.transpose(bank[:, r, :], turned_of[k][:, P * r : P * (r + 1)], ident[:])

        def add(k):
            bias = b1_all[:, ROWS1 * k : ROWS1 * (k + 1)].unsqueeze(1)
            nc.vector.tensor_tensor(
                out=out_rows[:, :, ROWS1 * k : ROWS1 * (k + 1)],
                in0=acc_of[k][:],
                in1=bias.to_broadcast([P, BATCH_TILES, ROWS1]),
                op=ADD,
            )

        def finish(k):
            part = out_rows[:, :, ROWS1 * k : ROWS1 * (k + 1)]
            if is_turned(k):
                nc.scalar.copy(out=part, in_=back_of[k][:])
            else:
                nc.scalar.activation(out=part, in_=part, func=RELU)
            if k + 1 in STORE_ENDS:
                first = max(end for end in STORE_ENDS if end <= k)
                cols = slice(ROWS1 * first, ROWS1 * (k + 1))
                nc.sync.dma_start(out=out_view[:, :, cols], in_=out_rows[:, :, cols])

        x_rows = const.tile([P, BATCH_TILES * D0], BF16)
        nc.sync.dma_start(out=x_rows[:], in_=x.rearrange("(q r) k -> q (r k)", r=BATCH_TILES))
        out_view = out.rearrange("(q r) d -> q r d", r=BATCH_TILES)
        out_rows = const.tile([P, BATCH_TILES, D2], F32)

        b0_rows = const.tile([P, K_PASS], BF16)
        b1_rows = const.tile([P, P], BF16)
        nc.vector.memset(b0_rows[:], 0.0)
        nc.vector.memset(b1_rows[:], 0.0)
        for i in range(AHEAD):
            load(i)
            if i == 1:
                nc.sync.dma_start(out=b0_rows[0:PASSES1, :], in_=b0.rearrange("(g c) -> g c", c=K_PASS))
                nc.sync.dma_start(out=b1_rows[0:UNITS1, :], in_=b1.rearrange("(k c) -> k c", c=ROWS1))

        ident = const.tile([P, P], F32)
        make_identity(nc, ident[:])
        ident_bf16 = const.tile([P, P], BF16)
        make_identity(nc, ident_bf16[:])
        multiply(0)

        x_words = x_rows[:].bitcast(F32).rearrange("q (r w) -> q r w", r=BATCH_TILES)
        x_grouped = const.tile([P, PASSES0 * BATCH * PACK], BF16, align_bytes=64)
        x_grouped_words = x_grouped[:].bitcast(F32).rearrange(
            "p (g r q u) -> p g r q u", g=PASSES0, r=BATCH_TILES, u=2
        )
        for r in range(BATCH_TILES):
            bank = tr_psum.tile([P, 4, P], F32, tag="tr")
            for s in range(4):
                g, u = divmod(s, 2)
                words = slice(2 * P * g + u, 2 * P * (g + 1), 2)
                nc.tensor.transpose(bank[:, s, :], x_words[:, r, words], ident[:])
            nc.scalar.copy(
                out=x_grouped_words[:, :, r, :, :],
                in_=bank[:].rearrange("p (g u) q -> p g q u", u=2),
            )
        x_codes = const.tile([P, PASSES0 * BATCH], U32, align_bytes=64)
        x_scales = const.tile([P, PASSES0 * BATCH], U8, align_bytes=64)

        b0_cols = const.tile([P, D1 // P], F32)
        b1_cols = const.tile([P, UNITS1], F32)

        def bias_columns():
            b0_words = b0_rows[:].bitcast(F32)
            b0_bank = tr_psum.tile([P, BANK], F32, tag="tr")
            for u in range(2):
                nc.tensor.transpose(
                    b0_bank[:, P * u : P * (u + 1)], b0_words[:, u : 2 * P : 2], ident[:]
                )
            b0_pairs = b0_bank[:, 0 : 2 * P].bitcast(BF16).rearrange("p (u g e) -> p u g e", u=2, e=2)
            nc.vector.tensor_copy(
                out=b0_cols[:].rearrange("p (g u e) -> p u g e", u=2, e=2),
                in_=b0_pairs[:, :, 0:PASSES1, :],
            )

            b1_bank = acc_psum.tile([P, BANK], F32, tag="acc")
            nc.tensor.matmul(
                b1_bank[:, 0:P], lhsT=b1_rows[:], rhs=ident_bf16[:], start=True, stop=True
            )
            nc.vector.tensor_copy(out=b1_cols[:], in_=b1_bank[:, 0:UNITS1])

        b1_all = const.tile([P, D2], F32)

        def last_unit():
            k = UNITS1 - 1
            codes, scales = codes_of[UNITS0 + k], scales_of[UNITS0 + k]
            cols = slice(ROWS1 * k, ROWS1 * (k + 1))
            half = BATCH_TILES // 2
            bias = b1_all[:, cols].unsqueeze(1).to_broadcast([P, half, ROWS1])
            for tiles in (slice(0, half), slice(half, BATCH_TILES)):
                acc = acc_psum.tile([P, half, ROWS1], F32, tag="acc")
                for r in range(tiles.start, tiles.stop):
                    for g in range(PASSES1):
                        h_cols = slice(BATCH * g + P * r, BATCH * g + P * (r + 1))
                        w_cols = slice(ROWS1 * g, ROWS1 * (g + 1))
                        nc.tensor.matmul_mx(
                            out=acc[:, r - tiles.start, :],
                            lhsT=h_codes[:, h_cols].bitcast(FP8X4),
                            lhsT_scale=h_scales[:, h_cols],
                            rhs=codes[:, w_cols].bitcast(FP8X4),
                            rhs_scale=scales[:, w_cols],
                            start=(g == 0),
                            stop=(g == PASSES1 - 1),
                        )
                part = out_rows[:, tiles, cols]
                nc.vector.tensor_tensor(out=part, in0=acc[:], in1=bias, op=ADD)
                nc.scalar.activation(out=part, in_=part, func=RELU)
                nc.sync.dma_start(out=out_view[:, tiles, cols], in_=part)

        def spread_b1(k):
            b1_bank = tr_psum.tile([P, BANK], F32, tag="tr")
            nc.tensor.matmul(
                b1_bank[:, 0:ROWS1],
                lhsT=ident_bf16[:, k : k + 1].to_broadcast([P, P]),
                rhs=b1_rows[:],
                start=True,
                stop=True,
            )
            nc.scalar.copy(
                out=b1_all[:, ROWS1 * k : ROWS1 * (k + 1)], in_=b1_bank[:, 0:ROWS1]
            )

        h_codes = const.tile([P, PASSES1 * BATCH], U32, align_bytes=64)
        h_scales = const.tile([P, PASSES1 * BATCH], U8, align_bytes=64)

        for s in range(UNITS + LAG_FINISH1):
            k_mx = s - LAG_MATMUL1 - UNITS0
            k_out = s - LAG_FINISH1 - UNITS0
            if s + AHEAD < UNITS:
                load(s + AHEAD)
            if 0 <= k_out < UNITS1 and is_turned(k_out):
                turn_back(k_out)
            if 0 <= k_out < UNITS1 - 1 and is_turned(k_out):
                finish(k_out)
            if 0 < s < UNITS:
                multiply(s)
            if s < UNITS:
                transpose(s)
            if s == 1:
                nc.vector.quantize_mx(
                    out=x_codes[:].bitcast(FP8X4), scales=x_scales[:], in_=x_grouped[:]
                )
            if 0 <= s - LAG_GROUP0 < UNITS0:
                layer0_group(s - LAG_GROUP0)
            if 0 <= s - LAG_QUANTISE0 < UNITS0:
                quantise(s - LAG_QUANTISE0)
            if s == 1:
                bias_columns()
            if UNITS0 <= s - LAG_QUANTISE1 < UNITS:
                quantise(s - LAG_QUANTISE1)
            if UNITS0 <= s - 1 < UNITS and not is_turned(s - 1 - UNITS0):
                spread_b1(s - 1 - UNITS0)
            if 0 <= s - LAG_GROUP0 < UNITS0:
                layer0_quantise(s - LAG_GROUP0)
            if 0 <= k_out < UNITS1 - 1 and not is_turned(k_out):
                add(k_out)
                finish(k_out)
            if 0 <= s - LAG_MATMUL0 < UNITS0:
                layer0_matmuls(s - LAG_MATMUL0)
            if 0 <= k_mx < UNITS1 - 1:
                layer1_matmuls(k_mx)
                if is_turned(k_mx):
                    turned_relu(k_mx)
            if s == UNITS + LAG_FINISH1 - 2:
                last_unit()
